import numpy as np
import ml_dtypes


def mxq(x, axis, fmt="e4m3"):
    dtype, down = {"e4m3": (ml_dtypes.float8_e4m3fn, 7), "e5m2": (ml_dtypes.float8_e5m2, 14)}[fmt]
    v = np.moveaxis(np.asarray(x, np.float32).astype(ml_dtypes.bfloat16).astype(np.float64), axis, -1)
    blocks = v.reshape(v.shape[:-1] + (-1, 32))
    amax = np.abs(blocks).max(-1, keepdims=True)
    byte = np.maximum(np.where(amax > 0, np.frexp(amax)[1] - 1 + 127, 0) - down, 1)
    scale = np.exp2(byte - 127.0)
    codes = (blocks / scale).astype(np.float32).astype(dtype).astype(np.float64)
    return np.moveaxis((codes * scale).reshape(v.shape), -1, axis)


WIDE = False


def mx_kscale(k):
    if not WIDE:
        return np.ones(k)
    levels = np.array([10, -10, 5, -5, 0])
    a = np.random.permutation(np.resize(levels, k // 512 * 4)).reshape(k // 512, 4)
    idx = np.arange(k)
    return np.exp2(a[idx // 512, idx % 128 // 32])


BF16 = ml_dtypes.bfloat16


def bf(x):
    return np.asarray(x, np.float32).astype(BF16)


def f64(x):
    return np.asarray(x).astype(np.float64)


E2M1 = np.array([0.0, 0.5, 1.0, 1.5, 2.0, 3.0, 4.0, 6.0, -0.0, -0.5, -1.0, -1.5, -2.0, -3.0, -4.0, -6.0])


def pack_weight(w, fmt):
    k, n = w.shape
    w = f64(bf(w)).reshape(k // 32, 32, n)
    amax = np.abs(w).max(1)
    if fmt == "e4m3":
        byte = np.frexp(amax)[1] - 1 + 127 - 7
    else:
        mant, ex = np.frexp(amax / 6.0)
        byte = np.where(mant > 0.5, ex, ex - 1) + 127
    byte = np.clip(np.where(amax > 0, byte, 1), 1, 254)
    scaled = (w * np.exp2(127.0 - byte)[:, None, :]).reshape(k, n).astype(np.float32)
    by_word = np.ascontiguousarray(scaled.reshape(k // 512, 128, 4, n).transpose(0, 1, 3, 2))
    if fmt == "e4m3":
        words = by_word.astype(ml_dtypes.float8_e4m3fn).view(np.uint8)
    else:
        c = by_word.astype(ml_dtypes.float4_e2m1fn).view(np.uint8) & 0xF
        words = c[..., 0::2] | (c[..., 1::2] << 4)
    return np.ascontiguousarray(words), np.ascontiguousarray(byte.astype(np.uint8).reshape(k // 512, 16, n))


def unpack_weight(words, scales, fmt):
    g, p, n, _ = words.shape
    if fmt == "e4m3":
        vals = np.ascontiguousarray(words).view(ml_dtypes.float8_e4m3fn).astype(np.float64)
    else:
        nib = np.empty((g, p, n, 4), np.uint8)
        nib[..., 0::2] = words & 0xF
        nib[..., 1::2] = words >> 4
        vals = E2M1[nib]
    vals = vals * np.repeat(np.exp2(scales.astype(np.float64) - 127.0), 8, axis=1)[..., None]
    return vals.transpose(0, 1, 3, 2).reshape(g * 512, n)


N, I, O = 128, 4096, 2048
FMT = "e4m3"


def setup_inputs():
    s = mx_kscale(I)
    mask = np.tile(np.array([0.0, 0.0, 1.0, 1.0]), I // 4)
    gd = mask + 0.1 * (1.0 - mask)
    gs = (1.0 - mask) + 0.1 * mask
    x = np.random.standard_normal((N, I)) * s
    wd = np.random.standard_normal((O, I)) * gd / np.sqrt(I) / s
    ws = np.random.standard_normal((O, I)) * gs / np.sqrt(I) / s
    wd_words, wd_scales = pack_weight(np.ascontiguousarray(wd.T), FMT)
    ws_words, ws_scales = pack_weight(np.ascontiguousarray(ws.T), FMT)
    return {"x": bf(x), "W_dense_words": wd_words, "W_dense_scales": wd_scales, "W_sparse_words": ws_words, "W_sparse_scales": ws_scales}


def reference(x, W_dense_words, W_dense_scales, W_sparse_words, W_sparse_scales):
    xq = mxq(f64(x), 1, "e4m3")
    out_dense = xq @ unpack_weight(W_dense_words, W_dense_scales, FMT)
    out_sparse = xq @ unpack_weight(W_sparse_words, W_sparse_scales, FMT)
    return out_dense + out_sparse

@@ -1,0 +1,119 @@
+from contextlib import ExitStack
+
+import concourse.mybir as mybir
+from concourse.masks import make_identity
+
+BF16 = mybir.dt.bfloat16
+F32 = mybir.dt.float32
+I32 = mybir.dt.int32
+U32 = mybir.dt.uint32
+U8 = mybir.dt.uint8
+FP8X4 = mybir.dt.float8_e4m3fn_x4
+
+P = 128
+PACK = 4
+K_PASS = P * PACK
+TOKENS = 128
+K = 4096
+N_OUT = 2048
+GROUPS = K // K_PASS
+N_BLOCK = 512
+BLOCKS = N_OUT // N_BLOCK
+QUADRANTS = 4
+ROWS = 4
+SHARE = 4
+WORDS_PER_GROUP = K_PASS // 2
+
+FLOPS = 2 * 2 * TOKENS * K * N_OUT
+
+
+def tile_myinterleavedmodule_w_kernel(
+    tc, x, W_dense_words, W_dense_scales, W_sparse_words, W_sparse_scales, out
+):
+    nc = tc.nc
+    weight_words = [W_dense_words, W_sparse_words]
+    weight_scales = [W_dense_scales, W_sparse_scales]
+    chunks = [(w, g) for w in range(2) for g in range(GROUPS)]
+    last = len(chunks) - 1
+
+    with ExitStack() as ctx:
+        keep = ctx.enter_context(tc.tile_pool(name="keep", bufs=1))
+        psum_x = ctx.enter_context(tc.psum_pool(name="psum_x", bufs=4))
+        psum_acc = ctx.enter_context(tc.psum_pool(name="psum_acc", bufs=1))
+
+        x_sb = keep.tile([P, K], BF16)
+        ident = keep.tile([P, P], F32)
+        grouped = keep.tile([P, GROUPS, TOKENS, PACK], BF16, align_bytes=64)
+        x_codes = keep.tile([P, GROUPS, TOKENS], U32, align_bytes=64)
+        x_scales = keep.tile([P, GROUPS, TOKENS], U8, align_bytes=64)
+        words = [keep.tile([P, N_OUT], U32, name="words%d" % c, align_bytes=64) for c in range(len(chunks))]
+        planes = keep.tile([P, len(chunks) // SHARE, N_OUT], U8, align_bytes=64)
+        acc = [psum_acc.tile([P, N_BLOCK], F32, name="acc%d" % j) for j in range(BLOCKS)]
+
+        nc.vector.memset(planes[:].rearrange("p s n -> p (s n)").bitcast(I32), 0)
+        make_identity(nc, ident[:])
+
+        nc.sync.dma_start(out=x_sb[:], in_=x)
+        for w in range(2):
+            for half in range(GROUPS // SHARE):
+                s = w * (GROUPS // SHARE) + half
+                for quad in range(QUADRANTS):
+                    nc.sync.dma_start(
+                        out=planes[32 * quad : 32 * quad + SHARE * ROWS, s, :].bitcast(I32),
+                        in_=weight_scales[w][
+                            SHARE * half : SHARE * (half + 1), ROWS * quad : ROWS * (quad + 1), :
+                        ].bitcast(I32),
+                    )
+        for c, (w, g) in enumerate(chunks):
+            chunk_in_hbm = weight_words[w][g].rearrange("p n t -> p (n t)").bitcast(I32)
+            cuts = BLOCKS if c == last else 1
+            width = N_OUT // cuts
+            for i in range(cuts):
+                cols = slice(i * width, (i + 1) * width)
+                nc.sync.dma_start(out=words[c][:, cols].bitcast(I32), in_=chunk_in_hbm[:, cols])
+
+        x_words = x_sb[:].bitcast(F32)
+        for pair in range(GROUPS // 2):
+            xt = psum_x.tile([P, 2, 2, TOKENS], F32)
+            for gi in range(2):
+                first = (2 * pair + gi) * WORDS_PER_GROUP
+                for u in range(2):
+                    nc.tensor.transpose(
+                        xt[:, gi, u, :], x_words[:, first + u : first + WORDS_PER_GROUP : 2], ident[:]
+                    )
+            side_by_side = grouped[:, 2 * pair : 2 * pair + 2].bitcast(F32)
+            by_token = xt[:].rearrange("p g u r -> p g r u")
+            if pair % 2 == 0:
+                nc.vector.tensor_copy(out=side_by_side, in_=by_token)
+            else:
+                nc.scalar.copy(out=side_by_side, in_=by_token)
+        for pair in range(GROUPS // 2):
+            gs = slice(2 * pair, 2 * pair + 2)
+            nc.vector.quantize_mx(
+                out=x_codes[:, gs, :].rearrange("p g r -> p (g r)").bitcast(FP8X4),
+                scales=x_scales[:, gs, :].rearrange("p g r -> p (g r)"),
+                in_=grouped[:, gs].rearrange("p g r t -> p (g r t)"),
+            )
+
+        for c, (w, g) in enumerate(chunks):
+            s = w * (GROUPS // SHARE) + g // SHARE
+            top = ROWS * (g % SHARE)
+            for j in range(BLOCKS):
+                cols = slice(j * N_BLOCK, (j + 1) * N_BLOCK)
+                nc.tensor.matmul_mx(
+                    out=acc[j][:],
+                    lhsT=x_codes[:, g, :].bitcast(FP8X4),
+                    lhsT_scale=x_scales[:, g, :],
+                    rhs=words[c][:, cols].bitcast(FP8X4),
+                    rhs_scale=planes[top:P, s, cols],
+                    start=(c == 0),
+                    stop=(c == last),
+                )
+
+        for j in range(BLOCKS):
+            result = keep.tile([P, N_BLOCK], F32, name="result%d" % j)
+            if j % 2 == 0:
+                nc.vector.tensor_copy(out=result[:], in_=acc[j][:])
+            else:
+                nc.scalar.copy(out=result[:], in_=acc[j][:])
+            nc.sync.dma_start(out=out[:, j * N_BLOCK : (j + 1) * N_BLOCK], in_=result[:])

@@ -58,11 +58,11 @@ def tile_myinterleavedmodule_w_kernel(
             for half in range(GROUPS // SHARE):
                 s = w * (GROUPS // SHARE) + half
                 for quad in range(QUADRANTS):
-                    nc.sync.dma_start(
-                        out=planes[32 * quad : 32 * quad + SHARE * ROWS, s, :].bitcast(I32),
+                    nc.gpsimd.dma_start(
+                        out=planes[32 * quad : 32 * quad + SHARE * ROWS, s, :].bitcast(F32),
                         in_=weight_scales[w][
                             SHARE * half : SHARE * (half + 1), ROWS * quad : ROWS * (quad + 1), :
-                        ].bitcast(I32),
+                        ].bitcast(F32),
                     )
         for c, (w, g) in enumerate(chunks):
             chunk_in_hbm = weight_words[w][g].rearrange("p n t -> p (n t)").bitcast(I32)

@@ -17,8 +17,7 @@ TOKENS = 128
 K = 4096
 N_OUT = 2048
 GROUPS = K // K_PASS
-N_BLOCK = 512
-BLOCKS = N_OUT // N_BLOCK
+BLOCK_COLS = [slice(0, 512), slice(512, 1024), slice(1024, 1536), slice(1536, 1792), slice(1792, 2048)]
 QUADRANTS = 4
 ROWS = 4
 SHARE = 4
@@ -38,7 +37,7 @@ def tile_myinterleavedmodule_w_kernel(
 
     with ExitStack() as ctx:
         keep = ctx.enter_context(tc.tile_pool(name="keep", bufs=1))
-        psum_x = ctx.enter_context(tc.psum_pool(name="psum_x", bufs=4))
+        psum_x = ctx.enter_context(tc.psum_pool(name="psum_x", bufs=3))
         psum_acc = ctx.enter_context(tc.psum_pool(name="psum_acc", bufs=1))
 
         x_sb = keep.tile([P, K], BF16)
@@ -48,7 +47,9 @@ def tile_myinterleavedmodule_w_kernel(
         x_scales = keep.tile([P, GROUPS, TOKENS], U8, align_bytes=64)
         words = [keep.tile([P, N_OUT], U32, name="words%d" % c, align_bytes=64) for c in range(len(chunks))]
         planes = keep.tile([P, len(chunks) // SHARE, N_OUT], U8, align_bytes=64)
-        acc = [psum_acc.tile([P, N_BLOCK], F32, name="acc%d" % j) for j in range(BLOCKS)]
+        acc = [
+            psum_acc.tile([P, cols.stop - cols.start], F32, name="acc%d" % j) for j, cols in enumerate(BLOCK_COLS)
+        ]
 
         nc.vector.memset(planes[:].rearrange("p s n -> p (s n)").bitcast(I32), 0)
         make_identity(nc, ident[:])
@@ -66,10 +67,7 @@ def tile_myinterleavedmodule_w_kernel(
                     )
         for c, (w, g) in enumerate(chunks):
             chunk_in_hbm = weight_words[w][g].rearrange("p n t -> p (n t)").bitcast(I32)
-            cuts = BLOCKS if c == last else 1
-            width = N_OUT // cuts
-            for i in range(cuts):
-                cols = slice(i * width, (i + 1) * width)
+            for cols in BLOCK_COLS if c == last else [slice(0, N_OUT)]:
                 nc.sync.dma_start(out=words[c][:, cols].bitcast(I32), in_=chunk_in_hbm[:, cols])
 
         x_words = x_sb[:].bitcast(F32)
@@ -98,8 +96,7 @@ def tile_myinterleavedmodule_w_kernel(
         for c, (w, g) in enumerate(chunks):
             s = w * (GROUPS // SHARE) + g // SHARE
             top = ROWS * (g % SHARE)
-            for j in range(BLOCKS):
-                cols = slice(j * N_BLOCK, (j + 1) * N_BLOCK)
+            for j, cols in enumerate(BLOCK_COLS):
                 nc.tensor.matmul_mx(
                     out=acc[j][:],
                     lhsT=x_codes[:, g, :].bitcast(FP8X4),
@@ -110,10 +107,10 @@ def tile_myinterleavedmodule_w_kernel(
                     stop=(c == last),
                 )
 
-        for j in range(BLOCKS):
-            result = keep.tile([P, N_BLOCK], F32, name="result%d" % j)
+        for j, cols in enumerate(BLOCK_COLS):
+            result = keep.tile([P, cols.stop - cols.start], F32, name="result%d" % j)
             if j % 2 == 0:
                 nc.vector.tensor_copy(out=result[:], in_=acc[j][:])
             else:
                 nc.scalar.copy(out=result[:], in_=acc[j][:])
-            nc.sync.dma_start(out=out[:, j * N_BLOCK : (j + 1) * N_BLOCK], in_=result[:])
+            nc.sync.dma_start(out=out[:, cols], in_=result[:])

@@ -20,6 +20,7 @@ GROUPS = K // K_PASS
 BLOCK_COLS = [slice(0, 512), slice(512, 1024), slice(1024, 1536), slice(1536, 1792), slice(1792, 2048)]
 QUADRANTS = 4
 ROWS = 4
+LATE_CHUNKS = 5
 SHARE = 4
 WORDS_PER_GROUP = K_PASS // 2
 
@@ -65,10 +66,14 @@ def tile_myinterleavedmodule_w_kernel(
                             SHARE * half : SHARE * (half + 1), ROWS * quad : ROWS * (quad + 1), :
                         ].bitcast(F32),
                     )
-        for c, (w, g) in enumerate(chunks):
+        late_cols = slice(BLOCK_COLS[3].start, N_OUT)
+        late = range(len(chunks) - LATE_CHUNKS, len(chunks))
+        loads = [(c, slice(0, late_cols.start if c in late else N_OUT)) for c in range(len(chunks))]
+        loads += [(c, late_cols) for c in late if c != last] + [(last, cols) for cols in BLOCK_COLS[3:]]
+        for c, cols in loads:
+            w, g = chunks[c]
             chunk_in_hbm = weight_words[w][g].rearrange("p n t -> p (n t)").bitcast(I32)
-            for cols in BLOCK_COLS if c == last else [slice(0, N_OUT)]:
-                nc.sync.dma_start(out=words[c][:, cols].bitcast(I32), in_=chunk_in_hbm[:, cols])
+            nc.sync.dma_start(out=words[c][:, cols].bitcast(I32), in_=chunk_in_hbm[:, cols])
 
         x_words = x_sb[:].bitcast(F32)
         for pair in range(GROUPS // 2):
@@ -93,10 +98,13 @@ def tile_myinterleavedmodule_w_kernel(
                 in_=grouped[:, gs].rearrange("p g r t -> p (g r t)"),
             )
 
-        for c, (w, g) in enumerate(chunks):
+        for c, loaded in loads:
+            w, g = chunks[c]
             s = w * (GROUPS // SHARE) + g // SHARE
             top = ROWS * (g % SHARE)
             for j, cols in enumerate(BLOCK_COLS):
+                if cols.start < loaded.start or cols.stop > loaded.stop:
+                    continue
                 nc.tensor.matmul_mx(
                     out=acc[j][:],
                     lhsT=x_codes[:, g, :].bitcast(FP8X4),

@@ -22,6 +22,7 @@ QUADRANTS = 4
 ROWS = 4
 LATE_CHUNKS = 5
 SHARE = 4
+DMA_ALIGN = 1024
 WORDS_PER_GROUP = K_PASS // 2
 
 FLOPS = 2 * 2 * TOKENS * K * N_OUT
@@ -41,13 +42,13 @@ def tile_myinterleavedmodule_w_kernel(
         psum_x = ctx.enter_context(tc.psum_pool(name="psum_x", bufs=3))
         psum_acc = ctx.enter_context(tc.psum_pool(name="psum_acc", bufs=1))
 
-        x_sb = keep.tile([P, K], BF16)
+        x_sb = keep.tile([P, K], BF16, align_bytes=DMA_ALIGN)
         ident = keep.tile([P, P], F32)
         grouped = keep.tile([P, GROUPS, TOKENS, PACK], BF16, align_bytes=64)
         x_codes = keep.tile([P, GROUPS, TOKENS], U32, align_bytes=64)
         x_scales = keep.tile([P, GROUPS, TOKENS], U8, align_bytes=64)
-        words = [keep.tile([P, N_OUT], U32, name="words%d" % c, align_bytes=64) for c in range(len(chunks))]
-        planes = keep.tile([P, len(chunks) // SHARE, N_OUT], U8, align_bytes=64)
+        words = [keep.tile([P, N_OUT], U32, name="words%d" % c, align_bytes=DMA_ALIGN) for c in range(len(chunks))]
+        planes = keep.tile([P, len(chunks) // SHARE, N_OUT], U8, align_bytes=DMA_ALIGN)
         acc = [
             psum_acc.tile([P, cols.stop - cols.start], F32, name="acc%d" % j) for j, cols in enumerate(BLOCK_COLS)
         ]
@@ -116,7 +117,7 @@ def tile_myinterleavedmodule_w_kernel(
                 )
 
         for j, cols in enumerate(BLOCK_COLS):
-            result = keep.tile([P, cols.stop - cols.start], F32, name="result%d" % j)
+            result = keep.tile([P, cols.stop - cols.start], F32, name="result%d" % j, align_bytes=DMA_ALIGN)
             if j % 2 == 0:
                 nc.vector.tensor_copy(out=result[:], in_=acc[j][:])
             else:

@@ -17,7 +17,8 @@ TOKENS = 128
 K = 4096
 N_OUT = 2048
 GROUPS = K // K_PASS
-BLOCK_COLS = [slice(0, 512), slice(512, 1024), slice(1024, 1536), slice(1536, 1792), slice(1792, 2048)]
+BLOCK_COLS = [slice(0, 512), slice(512, 1024), slice(1024, 1536), slice(1536, 1792), slice(1792, 1920), slice(1920, 2048)]
+STORE_COLS = [slice(0, 1024)] + BLOCK_COLS[2:]
 QUADRANTS = 4
 ROWS = 4
 LATE_CHUNKS = 5
@@ -39,7 +40,7 @@ def tile_myinterleavedmodule_w_kernel(
 
     with ExitStack() as ctx:
         keep = ctx.enter_context(tc.tile_pool(name="keep", bufs=1))
-        psum_x = ctx.enter_context(tc.psum_pool(name="psum_x", bufs=3))
+        psum_x = ctx.enter_context(tc.psum_pool(name="psum_x", bufs=2))
         psum_acc = ctx.enter_context(tc.psum_pool(name="psum_acc", bufs=1))
 
         x_sb = keep.tile([P, K], BF16, align_bytes=DMA_ALIGN)
@@ -116,10 +117,16 @@ def tile_myinterleavedmodule_w_kernel(
                     stop=(c == last),
                 )
 
-        for j, cols in enumerate(BLOCK_COLS):
-            result = keep.tile([P, cols.stop - cols.start], F32, name="result%d" % j, align_bytes=DMA_ALIGN)
-            if j % 2 == 0:
-                nc.vector.tensor_copy(out=result[:], in_=acc[j][:])
-            else:
-                nc.scalar.copy(out=result[:], in_=acc[j][:])
-            nc.sync.dma_start(out=out[:, cols], in_=result[:])
+        for stored in STORE_COLS:
+            result = keep.tile(
+                [P, stored.stop - stored.start], F32, name="result%d" % stored.start, align_bytes=DMA_ALIGN
+            )
+            for j, cols in enumerate(BLOCK_COLS):
+                if cols.start < stored.start or cols.stop > stored.stop:
+                    continue
+                part = result[:, cols.start - stored.start : cols.stop - stored.start]
+                if j % 2 == 1:
+                    nc.vector.tensor_copy(out=part, in_=acc[j][:])
+                else:
+                    nc.scalar.copy(out=part, in_=acc[j][:])
+            nc.sync.dma_start(out=out[:, stored], in_=result[:])

@@ -19,6 +19,7 @@ N_OUT = 2048
 GROUPS = K // K_PASS
 BLOCK_COLS = [slice(0, 512), slice(512, 1024), slice(1024, 1536), slice(1536, 1792), slice(1792, 1920), slice(1920, 2048)]
 STORE_COLS = [slice(0, 1024)] + BLOCK_COLS[2:]
+STEP_WORDS = 16
 QUADRANTS = 4
 ROWS = 4
 LATE_CHUNKS = 5
@@ -58,16 +59,33 @@ def tile_myinterleavedmodule_w_kernel(
         make_identity(nc, ident[:])
 
         nc.sync.dma_start(out=x_sb[:], in_=x)
-        for w in range(2):
-            for half in range(GROUPS // SHARE):
-                s = w * (GROUPS // SHARE) + half
-                for quad in range(QUADRANTS):
-                    nc.gpsimd.dma_start(
-                        out=planes[32 * quad : 32 * quad + SHARE * ROWS, s, :].bitcast(F32),
-                        in_=weight_scales[w][
-                            SHARE * half : SHARE * (half + 1), ROWS * quad : ROWS * (quad + 1), :
-                        ].bitcast(F32),
-                    )
+        def load_scale_rows(queue, dtype, s, quad):
+            w, half = divmod(s, GROUPS // SHARE)
+            queue.dma_start(
+                out=planes[32 * quad : 32 * quad + SHARE * ROWS, s, :].bitcast(dtype),
+                in_=weight_scales[w][
+                    SHARE * half : SHARE * (half + 1), ROWS * quad : ROWS * (quad + 1), :
+                ].bitcast(dtype),
+            )
+
+        sets = len(chunks) // SHARE
+        sync_scale_loads = [(s, quad) for s in range(sets) for quad in (0, 1)]
+        gpsimd_scale_loads = [(s, quad) for s in range(sets) for quad in (2, 3)]
+        steps = keep.tile([P, len(gpsimd_scale_loads) + 1, STEP_WORDS], F32, align_bytes=64)
+
+        def step_engines(i, rows):
+            nc.gpsimd.dma_start(
+                out=steps[0:rows, i, :],
+                in_=weight_scales[0][0][0:rows, 64 * i : 64 * (i + 1)].bitcast(F32),
+            )
+
+        with tc.manual_schedule(engines={mybir.EngineType.Pool}):
+            step_engines(0, 8)
+            for i, (s, quad) in enumerate(gpsimd_scale_loads):
+                load_scale_rows(nc.gpsimd, F32, s, quad)
+                step_engines(i + 1, 12 if i + 1 < len(gpsimd_scale_loads) else 4)
+        for s, quad in sync_scale_loads[:2]:
+            load_scale_rows(nc.sync, I32, s, quad)
         late_cols = slice(BLOCK_COLS[3].start, N_OUT)
         late = range(len(chunks) - LATE_CHUNKS, len(chunks))
         loads = [(c, slice(0, late_cols.start if c in late else N_OUT)) for c in range(len(chunks))]
@@ -76,6 +94,8 @@ def tile_myinterleavedmodule_w_kernel(
             w, g = chunks[c]
             chunk_in_hbm = weight_words[w][g].rearrange("p n t -> p (n t)").bitcast(I32)
             nc.sync.dma_start(out=words[c][:, cols].bitcast(I32), in_=chunk_in_hbm[:, cols])
+            if cols.start == 0 and c + 2 < len(sync_scale_loads):
+                load_scale_rows(nc.sync, I32, *sync_scale_loads[c + 2])
 
         x_words = x_sb[:].bitcast(F32)
         for pair in range(GROUPS // 2):

@@ -71,19 +71,21 @@ def tile_myinterleavedmodule_w_kernel(
         sets = len(chunks) // SHARE
         sync_scale_loads = [(s, quad) for s in range(sets) for quad in (0, 1)]
         gpsimd_scale_loads = [(s, quad) for s in range(sets) for quad in (2, 3)]
-        steps = keep.tile([P, len(gpsimd_scale_loads) + 1, STEP_WORDS], F32, align_bytes=64)
+        steps = keep.tile([P, 2 * len(gpsimd_scale_loads) + 1, STEP_WORDS], F32, align_bytes=64)
 
-        def step_engines(i, rows):
+        def step_engines(i, engines):
             nc.gpsimd.dma_start(
-                out=steps[0:rows, i, :],
-                in_=weight_scales[0][0][0:rows, 64 * i : 64 * (i + 1)].bitcast(F32),
+                out=steps[0 : ROWS * engines, i, :],
+                in_=weight_scales[0][0:engines, 0:ROWS, 64 * i : 64 * (i + 1)].bitcast(F32),
             )
 
         with tc.manual_schedule(engines={mybir.EngineType.Pool}):
             step_engines(0, 8)
             for i, (s, quad) in enumerate(gpsimd_scale_loads):
                 load_scale_rows(nc.gpsimd, F32, s, quad)
-                step_engines(i + 1, 12 if i + 1 < len(gpsimd_scale_loads) else 4)
+                if i + 1 < len(gpsimd_scale_loads):
+                    step_engines(2 * i + 1, 8)
+                step_engines(2 * i + 2, 4)
         for s, quad in sync_scale_loads[:2]:
             load_scale_rows(nc.sync, I32, s, quad)
         late_cols = slice(BLOCK_COLS[3].start, N_OUT)

from contextlib import ExitStack

import concourse.mybir as mybir
from concourse.masks import make_identity

BF16 = mybir.dt.bfloat16
F32 = mybir.dt.float32
I32 = mybir.dt.int32
U32 = mybir.dt.uint32
U8 = mybir.dt.uint8
FP8X4 = mybir.dt.float8_e4m3fn_x4

P = 128
PACK = 4
K_PASS = P * PACK
TOKENS = 128
K = 4096
N_OUT = 2048
GROUPS = K // K_PASS
BLOCK_COLS = [slice(0, 512), slice(512, 1024), slice(1024, 1536), slice(1536, 1792), slice(1792, 1920), slice(1920, 2048)]
STORE_COLS = [slice(0, 1024)] + BLOCK_COLS[2:]
STEP_WORDS = 16
QUADRANTS = 4
ROWS = 4
LATE_CHUNKS = 5
SHARE = 4
DMA_ALIGN = 1024
WORDS_PER_GROUP = K_PASS // 2

FLOPS = 2 * 2 * TOKENS * K * N_OUT


def tile_myinterleavedmodule_w_kernel(
    tc, x, W_dense_words, W_dense_scales, W_sparse_words, W_sparse_scales, out
):
    nc = tc.nc
    weight_words = [W_dense_words, W_sparse_words]
    weight_scales = [W_dense_scales, W_sparse_scales]
    chunks = [(w, g) for w in range(2) for g in range(GROUPS)]
    last = len(chunks) - 1

    with ExitStack() as ctx:
        keep = ctx.enter_context(tc.tile_pool(name="keep", bufs=1))
        psum_x = ctx.enter_context(tc.psum_pool(name="psum_x", bufs=2))
        psum_acc = ctx.enter_context(tc.psum_pool(name="psum_acc", bufs=1))

        x_sb = keep.tile([P, K], BF16, align_bytes=DMA_ALIGN)
        ident = keep.tile([P, P], F32)
        grouped = keep.tile([P, GROUPS, TOKENS, PACK], BF16, align_bytes=64)
        x_codes = keep.tile([P, GROUPS, TOKENS], U32, align_bytes=64)
        x_scales = keep.tile([P, GROUPS, TOKENS], U8, align_bytes=64)
        words = [keep.tile([P, N_OUT], U32, name="words%d" % c, align_bytes=DMA_ALIGN) for c in range(len(chunks))]
        planes = keep.tile([P, len(chunks) // SHARE, N_OUT], U8, align_bytes=DMA_ALIGN)
        acc = [
            psum_acc.tile([P, cols.stop - cols.start], F32, name="acc%d" % j) for j, cols in enumerate(BLOCK_COLS)
        ]

        nc.vector.memset(planes[:].rearrange("p s n -> p (s n)").bitcast(I32), 0)
        make_identity(nc, ident[:])

        nc.sync.dma_start(out=x_sb[:], in_=x)
        def load_scale_rows(queue, dtype, s, quad):
            w, half = divmod(s, GROUPS // SHARE)
            queue.dma_start(
                out=planes[32 * quad : 32 * quad + SHARE * ROWS, s, :].bitcast(dtype),
                in_=weight_scales[w][
                    SHARE * half : SHARE * (half + 1), ROWS * quad : ROWS * (quad + 1), :
                ].bitcast(dtype),
            )

        sets = len(chunks) // SHARE
        sync_scale_loads = [(s, quad) for s in range(sets) for quad in (0, 1)]
        gpsimd_scale_loads = [(s, quad) for s in range(sets) for quad in (2, 3)]
        steps = keep.tile([P, 2 * len(gpsimd_scale_loads) + 1, STEP_WORDS], F32, align_bytes=64)

        def step_engines(i, engines):
            nc.gpsimd.dma_start(
                out=steps[0 : ROWS * engines, i, :],
                in_=weight_scales[0][0:engines, 0:ROWS, 64 * i : 64 * (i + 1)].bitcast(F32),
            )

        with tc.manual_schedule(engines={mybir.EngineType.Pool}):
            step_engines(0, 8)
            for i, (s, quad) in enumerate(gpsimd_scale_loads):
                load_scale_rows(nc.gpsimd, F32, s, quad)
                if i + 1 < len(gpsimd_scale_loads):
                    step_engines(2 * i + 1, 8)
                step_engines(2 * i + 2, 4)
        for s, quad in sync_scale_loads[:2]:
            load_scale_rows(nc.sync, I32, s, quad)
        late_cols = slice(BLOCK_COLS[3].start, N_OUT)
        late = range(len(chunks) - LATE_CHUNKS, len(chunks))
        loads = [(c, slice(0, late_cols.start if c in late else N_OUT)) for c in range(len(chunks))]
        loads += [(c, late_cols) for c in late if c != last] + [(last, cols) for cols in BLOCK_COLS[3:]]
        for c, cols in loads:
            w, g = chunks[c]
            chunk_in_hbm = weight_words[w][g].rearrange("p n t -> p (n t)").bitcast(I32)
            nc.sync.dma_start(out=words[c][:, cols].bitcast(I32), in_=chunk_in_hbm[:, cols])
            if cols.start == 0 and c + 2 < len(sync_scale_loads):
                load_scale_rows(nc.sync, I32, *sync_scale_loads[c + 2])

        x_words = x_sb[:].bitcast(F32)
        for pair in range(GROUPS // 2):
            xt = psum_x.tile([P, 2, 2, TOKENS], F32)
            for gi in range(2):
                first = (2 * pair + gi) * WORDS_PER_GROUP
                for u in range(2):
                    nc.tensor.transpose(
                        xt[:, gi, u, :], x_words[:, first + u : first + WORDS_PER_GROUP : 2], ident[:]
                    )
            side_by_side = grouped[:, 2 * pair : 2 * pair + 2].bitcast(F32)
            by_token = xt[:].rearrange("p g u r -> p g r u")
            if pair % 2 == 0:
                nc.vector.tensor_copy(out=side_by_side, in_=by_token)
            else:
                nc.scalar.copy(out=side_by_side, in_=by_token)
        for pair in range(GROUPS // 2):
            gs = slice(2 * pair, 2 * pair + 2)
            nc.vector.quantize_mx(
                out=x_codes[:, gs, :].rearrange("p g r -> p (g r)").bitcast(FP8X4),
                scales=x_scales[:, gs, :].rearrange("p g r -> p (g r)"),
                in_=grouped[:, gs].rearrange("p g r t -> p (g r t)"),
            )

        for c, loaded in loads:
            w, g = chunks[c]
            s = w * (GROUPS // SHARE) + g // SHARE
            top = ROWS * (g % SHARE)
            for j, cols in enumerate(BLOCK_COLS):
                if cols.start < loaded.start or cols.stop > loaded.stop:
                    continue
                nc.tensor.matmul_mx(
                    out=acc[j][:],
                    lhsT=x_codes[:, g, :].bitcast(FP8X4),
                    lhsT_scale=x_scales[:, g, :],
                    rhs=words[c][:, cols].bitcast(FP8X4),
                    rhs_scale=planes[top:P, s, cols],
                    start=(c == 0),
                    stop=(c == last),
                )

        for stored in STORE_COLS:
            result = keep.tile(
                [P, stored.stop - stored.start], F32, name="result%d" % stored.start, align_bytes=DMA_ALIGN
            )
            for j, cols in enumerate(BLOCK_COLS):
                if cols.start < stored.start or cols.stop > stored.stop:
                    continue
                part = result[:, cols.start - stored.start : cols.stop - stored.start]
                if j % 2 == 1:
                    nc.vector.tensor_copy(out=part, in_=acc[j][:])
                else:
                    nc.scalar.copy(out=part, in_=acc[j][:])
            nc.sync.dma_start(out=out[:, stored], in_=result[:])
